import numpy as np
import ml_dtypes


def mxq(x, axis, fmt="e4m3"):
    dtype, down = {"e4m3": (ml_dtypes.float8_e4m3fn, 7), "e5m2": (ml_dtypes.float8_e5m2, 14)}[fmt]
    v = np.moveaxis(np.asarray(x, np.float32).astype(ml_dtypes.bfloat16).astype(np.float64), axis, -1)
    blocks = v.reshape(v.shape[:-1] + (-1, 32))
    amax = np.abs(blocks).max(-1, keepdims=True)
    byte = np.maximum(np.where(amax > 0, np.frexp(amax)[1] - 1 + 127, 0) - down, 1)
    scale = np.exp2(byte - 127.0)
    codes = (blocks / scale).astype(np.float32).astype(dtype).astype(np.float64)
    return np.moveaxis((codes * scale).reshape(v.shape), -1, axis)


WIDE = False


def mx_kscale(k):
    if not WIDE:
        return np.ones(k)
    levels = np.array([10, -10, 5, -5, 0])
    a = np.random.permutation(np.resize(levels, k // 512 * 4)).reshape(k // 512, 4)
    idx = np.arange(k)
    return np.exp2(a[idx // 512, idx % 128 // 32])


BF16 = ml_dtypes.bfloat16


def bf(x):
    return np.asarray(x, np.float32).astype(BF16)


def f64(x):
    return np.asarray(x).astype(np.float64)


E2M1 = np.array([0.0, 0.5, 1.0, 1.5, 2.0, 3.0, 4.0, 6.0, -0.0, -0.5, -1.0, -1.5, -2.0, -3.0, -4.0, -6.0])


def pack_weight(w, fmt):
    k, n = w.shape
    w = f64(bf(w)).reshape(k // 32, 32, n)
    amax = np.abs(w).max(1)
    if fmt == "e4m3":
        byte = np.frexp(amax)[1] - 1 + 127 - 7
    else:
        mant, ex = np.frexp(amax / 6.0)
        byte = np.where(mant > 0.5, ex, ex - 1) + 127
    byte = np.clip(np.where(amax > 0, byte, 1), 1, 254)
    scaled = (w * np.exp2(127.0 - byte)[:, None, :]).reshape(k, n).astype(np.float32)
    by_word = np.ascontiguousarray(scaled.reshape(k // 512, 128, 4, n).transpose(0, 1, 3, 2))
    if fmt == "e4m3":
        words = by_word.astype(ml_dtypes.float8_e4m3fn).view(np.uint8)
    else:
        c = by_word.astype(ml_dtypes.float4_e2m1fn).view(np.uint8) & 0xF
        words = c[..., 0::2] | (c[..., 1::2] << 4)
    return np.ascontiguousarray(words), np.ascontiguousarray(byte.astype(np.uint8).reshape(k // 512, 16, n))


def unpack_weight(words, scales, fmt):
    g, p, n, _ = words.shape
    if fmt == "e4m3":
        vals = np.ascontiguousarray(words).view(ml_dtypes.float8_e4m3fn).astype(np.float64)
    else:
        nib = np.empty((g, p, n, 4), np.uint8)
        nib[..., 0::2] = words & 0xF
        nib[..., 1::2] = words >> 4
        vals = E2M1[nib]
    vals = vals * np.repeat(np.exp2(scales.astype(np.float64) - 127.0), 8, axis=1)[..., None]
    return vals.transpose(0, 1, 3, 2).reshape(g * 512, n)


B, Q, D = 256, 2048, 512
COMBOS = ((0, 1), (0, 2), (0, 3), (1, 0), (1, 2), (2, 0), (2, 1), (3, 0))
T = 0.07
V = 1 + max(max(c) for c in COMBOS)
FMT = "e4m3"


def setup_inputs():
    s = mx_kscale(D)
    c = np.mean(s * s)
    shared = np.random.standard_normal((B, D))
    d = {}
    for v in range(V):
        gain = np.random.uniform(0.6, 1.6, (B, 1))
        own = np.random.standard_normal((B, D))
        d["x%d" % v] = bf((np.sqrt(0.1) * shared + np.sqrt(0.9) * own) * gain * s)
    for v in range(V):
        words, scales = pack_weight((np.random.standard_normal((Q, D)) * c / s).T, FMT)
        d["mem%d_words" % v] = words
        d["mem%d_scales" % v] = scales
    return d


def reference(x0, x1, x2, x3, mem0_words, mem0_scales, mem1_words, mem1_scales, mem2_words, mem2_scales, mem3_words, mem3_scales):
    X = [f64(x0), f64(x1), f64(x2), f64(x3)]
    Xn = [np.sqrt(np.sum(x * x, axis=1, keepdims=True)) for x in X]
    Xq = [mxq(x, 1, "e4m3") for x in X]
    Mq = [unpack_weight(w, sc, FMT).T for w, sc in ((mem0_words, mem0_scales), (mem1_words, mem1_scales), (mem2_words, mem2_scales), (mem3_words, mem3_scales))]
    outs = []
    for i, j in COMBOS:
        self_dot = np.sum(X[i] * X[j], axis=1, keepdims=True)
        mem_dot = Xq[i] @ Mq[j].T
        logits = np.concatenate([self_dot, mem_dot], axis=1)
        outs.append(np.exp(logits / (Xn[i] * Xn[j]) / T))
    return np.stack(outs)

@@ -1,0 +1,192 @@
+from contextlib import ExitStack
+
+import concourse.mybir as mybir
+from concourse.masks import make_identity
+
+F32 = mybir.dt.float32
+BF16 = mybir.dt.bfloat16
+I32 = mybir.dt.int32
+U32 = mybir.dt.uint32
+U8 = mybir.dt.uint8
+FP8X4 = mybir.dt.float8_e4m3fn_x4
+ACT = mybir.ActivationFunctionType
+ALU = mybir.AluOpType
+
+P = 128
+BATCH, BANK_ROWS, FEATURES = 256, 2048, 512
+VIEWS = 4
+COMBOS = ((0, 1), (0, 2), (0, 3), (1, 0), (1, 2), (2, 0), (2, 1), (3, 0))
+TEMPERATURE = 0.07
+
+ROWS = BATCH // P
+PACK = 4
+WORD_HALVES = 2
+N_TILE = 512
+N_TILES = BANK_ROWS // N_TILE
+QUADRANT = 32
+SCALE_ROWS = 4
+BLOCK_F32 = 8
+
+FLOPS = 2 * len(COMBOS) * BATCH * BANK_ROWS * FEATURES
+
+
+def tile_memorymoco_pa_kernel(
+    tc,
+    x0, x1, x2, x3,
+    mem0_words, mem0_scales, mem1_words, mem1_scales,
+    mem2_words, mem2_scales, mem3_words, mem3_scales,
+    out,
+):
+    nc = tc.nc
+    views = (x0, x1, x2, x3)
+    bank_words = (mem0_words, mem1_words, mem2_words, mem3_words)
+    bank_scales = (mem0_scales, mem1_scales, mem2_scales, mem3_scales)
+
+    bank_order = []
+    pair_order = []
+    for i, j in COMBOS:
+        if j not in bank_order:
+            bank_order.append(j)
+        if (min(i, j), max(i, j)) not in pair_order:
+            pair_order.append((min(i, j), max(i, j)))
+
+    with ExitStack() as ctx:
+        keep = ctx.enter_context(tc.tile_pool(name="keep", bufs=1))
+        scratch = ctx.enter_context(tc.tile_pool(name="scratch", bufs=4))
+        results = ctx.enter_context(tc.tile_pool(name="results", bufs=len(COMBOS)))
+        psum_x = ctx.enter_context(tc.psum_pool(name="psum_x", bufs=VIEWS))
+        psum_acc = ctx.enter_context(tc.psum_pool(name="psum_acc", bufs=4))
+        ctx.enter_context(tc.manual_schedule())
+
+        planes = keep.tile([P, VIEWS, BANK_ROWS], U8, name="planes", align_bytes=64)
+        planes_i32 = planes[:].bitcast(I32)
+
+        one = keep.tile([P, 1], F32, name="one")
+        nc.vector.memset(one[:], 1.0)
+        warm = keep.tile([P, 1], F32, name="warm")
+        nc.scalar.activation(out=warm[:], in_=one[:], func=ACT.Sqrt)
+
+        ident = keep.tile([P, P], F32, name="ident")
+        make_identity(nc, ident[:])
+
+        x_sb = []
+        for v in range(VIEWS):
+            x_tile = keep.tile([P, ROWS, FEATURES], BF16, name="x%d" % v)
+            nc.sync.dma_start(out=x_tile[:], in_=views[v].rearrange("(p r) d -> p r d", r=ROWS))
+            x_sb.append(x_tile)
+
+        w_sb = {}
+        for j in bank_order:
+            nc.vector.memset(planes_i32[:, j, :], 0)
+            rows_by_s = bank_scales[j][0].rearrange("(q s) n -> s q n", s=SCALE_ROWS)
+            for s in range(SCALE_ROWS):
+                nc.sync.dma_start(
+                    out=planes_i32[s : P : QUADRANT, j, :],
+                    in_=rows_by_s[s].bitcast(I32),
+                )
+            w_tile = keep.tile([P, BANK_ROWS], I32, name="w%d" % j, align_bytes=64)
+            nc.sync.dma_start(
+                out=w_tile[:], in_=bank_words[j][0].rearrange("p n t -> p (n t)").bitcast(I32)
+            )
+            w_sb[j] = w_tile
+
+        x_t = []
+        for v in range(VIEWS):
+            xt = psum_x.tile([P, ROWS, WORD_HALVES, P], F32, name="xt")
+            x_words = x_sb[v][:].bitcast(F32)
+            for r in range(ROWS):
+                for u in range(WORD_HALVES):
+                    nc.tensor.transpose(
+                        xt[:, r, u, :], x_words[:, r, u : FEATURES // 2 : WORD_HALVES], ident[:]
+                    )
+            x_t.append(xt)
+
+        sumsq = keep.tile([P, ROWS, BLOCK_F32], F32, name="sumsq")
+        for v in range(VIEWS):
+            squares = scratch.tile([P, FEATURES], F32, name="squares")
+            nc.scalar.activation(
+                out=squares[:], in_=x_sb[v][:, 0, :], func=ACT.Square, accum_out=sumsq[:, 0, v : v + 1]
+            )
+            products = scratch.tile([P, FEATURES], F32, name="products")
+            nc.vector.scalar_tensor_tensor(
+                out=products[:], in0=x_sb[v][:, 1, :], scalar=1.0, in1=x_sb[v][:, 1, :],
+                op0=ALU.mult, op1=ALU.mult, accum_out=sumsq[:, 1, v : v + 1],
+            )
+
+        x_codes = []
+        x_planes = []
+
+        def quantise_view(v):
+            grouped = scratch.tile([P, ROWS * P * PACK], BF16, name="grouped", align_bytes=64)
+            nc.vector.tensor_copy(
+                out=grouped[:].bitcast(F32).rearrange("p (r b u) -> p r b u", r=ROWS, u=WORD_HALVES),
+                in_=x_t[v][:].rearrange("p r u b -> p r b u"),
+            )
+            codes = keep.tile([P, ROWS * P], U32, name="x_codes%d" % v, align_bytes=64)
+            plane = keep.tile([P, ROWS * P], U8, name="x_plane%d" % v, align_bytes=64)
+            nc.vector.quantize_mx(out=codes[:].bitcast(FP8X4), scales=plane[:], in_=grouped[:])
+            x_codes.append(codes)
+            x_planes.append(plane)
+
+        quantise_view(0)
+
+        lengths = keep.tile([P, ROWS, VIEWS], F32, name="lengths")
+        nc.scalar.activation(
+            out=lengths[:], in_=sumsq[:, :, 0:VIEWS], func=ACT.Sqrt, scale=TEMPERATURE
+        )
+        nc.scalar.activation(out=warm[:], in_=one[:], func=ACT.Exp)
+        inverse = keep.tile([P, ROWS, VIEWS], F32, name="inverse")
+        nc.vector.reciprocal(out=inverse[:], in_=lengths[:])
+        row_scale = {}
+        for a, b in pair_order:
+            pair_scale = keep.tile([P, ROWS], F32, name="scale%d%d" % (a, b))
+            nc.vector.tensor_tensor(
+                out=pair_scale[:], in0=inverse[:, :, a], in1=inverse[:, :, b], op=ALU.mult
+            )
+            row_scale[(a, b)] = pair_scale
+
+        self_logit = {}
+        for a, b in pair_order:
+            dots = keep.tile([P, ROWS], F32, name="dots%d%d" % (a, b))
+            for r in range(ROWS):
+                products = scratch.tile([P, FEATURES], F32, name="products")
+                nc.vector.scalar_tensor_tensor(
+                    out=products[:], in0=x_sb[a][:, r, :], scalar=1.0, in1=x_sb[b][:, r, :],
+                    op0=ALU.mult, op1=ALU.mult, accum_out=dots[:, r : r + 1],
+                )
+            logit = keep.tile([P, ROWS], F32, name="logit%d%d" % (a, b))
+            nc.vector.tensor_tensor(out=logit[:], in0=dots[:], in1=row_scale[(a, b)][:], op=ALU.mult)
+            self_logit[(a, b)] = logit
+
+        for v in range(1, VIEWS):
+            quantise_view(v)
+
+        for c, (i, j) in enumerate(COMBOS):
+            pair = (min(i, j), max(i, j))
+            result = results.tile([P, ROWS, 1 + BANK_ROWS], F32, name="result")
+            for r in range(ROWS):
+                batch_cols = slice(r * P, (r + 1) * P)
+                for n in range(N_TILES):
+                    bank_cols = slice(n * N_TILE, (n + 1) * N_TILE)
+                    acc = psum_acc.tile([P, N_TILE], F32, name="acc")
+                    nc.tensor.matmul_mx(
+                        out=acc[:],
+                        lhsT=x_codes[i][:, batch_cols].bitcast(FP8X4),
+                        lhsT_scale=x_planes[i][:, batch_cols],
+                        rhs=w_sb[j][:, bank_cols].bitcast(FP8X4),
+                        rhs_scale=planes[:, j, bank_cols],
+                        start=True,
+                        stop=True,
+                    )
+                    nc.scalar.activation(
+                        out=result[:, r, 1 + n * N_TILE : 1 + (n + 1) * N_TILE],
+                        in_=acc[:],
+                        func=ACT.Exp,
+                        scale=row_scale[pair][:, r : r + 1],
+                    )
+                nc.scalar.activation(
+                    out=result[:, r, 0:1], in_=self_logit[pair][:, r : r + 1], func=ACT.Exp
+                )
+                nc.sync.dma_start(
+                    out=out[c].rearrange("(p r) q -> p r q", r=ROWS)[:, r, :], in_=result[:, r, :]
+                )

@@ -187,6 +187,7 @@ def tile_memorymoco_pa_kernel(
                 nc.scalar.activation(
                     out=result[:, r, 0:1], in_=self_logit[pair][:, r : r + 1], func=ACT.Exp
                 )
-                nc.sync.dma_start(
-                    out=out[c].rearrange("(p r) q -> p r q", r=ROWS)[:, r, :], in_=result[:, r, :]
-                )
+            nc.sync.dma_start(
+                out=out[c].rearrange("(p r) q -> p (r q)", r=ROWS),
+                in_=result[:].rearrange("p r q -> p (r q)"),
+            )

@@ -60,6 +60,7 @@ def tile_memorymoco_pa_kernel(
 
         planes = keep.tile([P, VIEWS, BANK_ROWS], U8, name="planes", align_bytes=64)
         planes_i32 = planes[:].bitcast(I32)
+        planes_f32 = planes[:].bitcast(F32)
 
         one = keep.tile([P, 1], F32, name="one")
         nc.vector.memset(one[:], 1.0)
@@ -80,9 +81,9 @@ def tile_memorymoco_pa_kernel(
             nc.vector.memset(planes_i32[:, j, :], 0)
             rows_by_s = bank_scales[j][0].rearrange("(q s) n -> s q n", s=SCALE_ROWS)
             for s in range(SCALE_ROWS):
-                nc.sync.dma_start(
-                    out=planes_i32[s : P : QUADRANT, j, :],
-                    in_=rows_by_s[s].bitcast(I32),
+                nc.gpsimd.dma_start(
+                    out=planes_f32[s : P : QUADRANT, j, :],
+                    in_=rows_by_s[s].bitcast(F32),
                 )
             w_tile = keep.tile([P, BANK_ROWS], I32, name="w%d" % j, align_bytes=64)
             nc.sync.dma_start(
@@ -187,7 +188,6 @@ def tile_memorymoco_pa_kernel(
                 nc.scalar.activation(
                     out=result[:, r, 0:1], in_=self_logit[pair][:, r : r + 1], func=ACT.Exp
                 )
-            nc.sync.dma_start(
-                out=out[c].rearrange("(p r) q -> p (r q)", r=ROWS),
-                in_=result[:].rearrange("p r q -> p (r q)"),
-            )
+                nc.sync.dma_start(
+                    out=out[c].rearrange("(p r) q -> p r q", r=ROWS)[:, r, :], in_=result[:, r, :]
+                )

@@ -58,10 +58,6 @@ def tile_memorymoco_pa_kernel(
         psum_acc = ctx.enter_context(tc.psum_pool(name="psum_acc", bufs=4))
         ctx.enter_context(tc.manual_schedule())
 
-        planes = keep.tile([P, VIEWS, BANK_ROWS], U8, name="planes", align_bytes=64)
-        planes_i32 = planes[:].bitcast(I32)
-        planes_f32 = planes[:].bitcast(F32)
-
         one = keep.tile([P, 1], F32, name="one")
         nc.vector.memset(one[:], 1.0)
         warm = keep.tile([P, 1], F32, name="warm")
@@ -77,14 +73,15 @@ def tile_memorymoco_pa_kernel(
             x_sb.append(x_tile)
 
         w_sb = {}
+        w_planes = {}
         for j in bank_order:
-            nc.vector.memset(planes_i32[:, j, :], 0)
+            plane = keep.tile([P, BANK_ROWS], U8, name="w_plane%d" % j, align_bytes=64)
+            plane_i32 = plane[:].bitcast(I32)
+            nc.vector.memset(plane_i32, 0)
             rows_by_s = bank_scales[j][0].rearrange("(q s) n -> s q n", s=SCALE_ROWS)
             for s in range(SCALE_ROWS):
-                nc.gpsimd.dma_start(
-                    out=planes_f32[s : P : QUADRANT, j, :],
-                    in_=rows_by_s[s].bitcast(F32),
-                )
+                nc.sync.dma_start(out=plane_i32[s : P : QUADRANT, :], in_=rows_by_s[s].bitcast(I32))
+            w_planes[j] = plane
             w_tile = keep.tile([P, BANK_ROWS], I32, name="w%d" % j, align_bytes=64)
             nc.sync.dma_start(
                 out=w_tile[:], in_=bank_words[j][0].rearrange("p n t -> p (n t)").bitcast(I32)
@@ -175,7 +172,7 @@ def tile_memorymoco_pa_kernel(
                         lhsT=x_codes[i][:, batch_cols].bitcast(FP8X4),
                         lhsT_scale=x_planes[i][:, batch_cols],
                         rhs=w_sb[j][:, bank_cols].bitcast(FP8X4),
-                        rhs_scale=planes[:, j, bank_cols],
+                        rhs_scale=w_planes[j][:, bank_cols],
                         start=True,
                         stop=True,
                     )

@@ -49,6 +49,7 @@ def tile_memorymoco_pa_kernel(
             bank_order.append(j)
         if (min(i, j), max(i, j)) not in pair_order:
             pair_order.append((min(i, j), max(i, j)))
+    n_pairs = len(pair_order)
 
     with ExitStack() as ctx:
         keep = ctx.enter_context(tc.tile_pool(name="keep", bufs=1))
@@ -61,20 +62,24 @@ def tile_memorymoco_pa_kernel(
         one = keep.tile([P, 1], F32, name="one")
         nc.vector.memset(one[:], 1.0)
         warm = keep.tile([P, 1], F32, name="warm")
-        nc.scalar.activation(out=warm[:], in_=one[:], func=ACT.Sqrt)
+        nc.scalar.activation(out=warm[:], in_=one[:], func=ACT.Exp)
+        neg_half = keep.tile([P, ROWS, VIEWS], F32, name="neg_half")
+        nc.vector.memset(neg_half[:], -0.5)
 
         ident = keep.tile([P, P], F32, name="ident")
         make_identity(nc, ident[:])
 
-        x_sb = []
-        for v in range(VIEWS):
+        x_sb = {}
+
+        def load_view(v):
             x_tile = keep.tile([P, ROWS, FEATURES], BF16, name="x%d" % v)
             nc.sync.dma_start(out=x_tile[:], in_=views[v].rearrange("(p r) d -> p r d", r=ROWS))
-            x_sb.append(x_tile)
+            x_sb[v] = x_tile
 
         w_sb = {}
         w_planes = {}
-        for j in bank_order:
+
+        def load_bank(j, chunks):
             plane = keep.tile([P, BANK_ROWS], U8, name="w_plane%d" % j, align_bytes=64)
             plane_i32 = plane[:].bitcast(I32)
             nc.vector.memset(plane_i32, 0)
@@ -82,14 +87,26 @@ def tile_memorymoco_pa_kernel(
             for s in range(SCALE_ROWS):
                 nc.sync.dma_start(out=plane_i32[s : P : QUADRANT, :], in_=rows_by_s[s].bitcast(I32))
             w_planes[j] = plane
-            w_tile = keep.tile([P, BANK_ROWS], I32, name="w%d" % j, align_bytes=64)
-            nc.sync.dma_start(
-                out=w_tile[:], in_=bank_words[j][0].rearrange("p n t -> p (n t)").bitcast(I32)
-            )
-            w_sb[j] = w_tile
+            words = bank_words[j][0].rearrange("p n t -> p (n t)").bitcast(I32)
+            first = 0
+            for tiles in chunks:
+                w_tile = keep.tile([P, tiles * N_TILE], I32, name="w%d_%d" % (j, first), align_bytes=64)
+                nc.sync.dma_start(out=w_tile[:], in_=words[:, first * N_TILE : (first + tiles) * N_TILE])
+                for n in range(tiles):
+                    w_sb[(j, first + n)] = w_tile[:, n * N_TILE : (n + 1) * N_TILE]
+                first += tiles
 
-        x_t = []
-        for v in range(VIEWS):
+        load_view(0)
+        load_view(1)
+        load_bank(bank_order[0], (1, 1, 2))
+        load_view(2)
+        load_view(3)
+        for j in bank_order[1:]:
+            load_bank(j, (N_TILES,))
+
+        x_t = {}
+
+        def transpose_view(v):
             xt = psum_x.tile([P, ROWS, WORD_HALVES, P], F32, name="xt")
             x_words = x_sb[v][:].bitcast(F32)
             for r in range(ROWS):
@@ -97,94 +114,166 @@ def tile_memorymoco_pa_kernel(
                     nc.tensor.transpose(
                         xt[:, r, u, :], x_words[:, r, u : FEATURES // 2 : WORD_HALVES], ident[:]
                     )
-            x_t.append(xt)
+            x_t[v] = xt
 
         sumsq = keep.tile([P, ROWS, BLOCK_F32], F32, name="sumsq")
-        for v in range(VIEWS):
+
+        def sumsq_scalar(v, r):
             squares = scratch.tile([P, FEATURES], F32, name="squares")
             nc.scalar.activation(
-                out=squares[:], in_=x_sb[v][:, 0, :], func=ACT.Square, accum_out=sumsq[:, 0, v : v + 1]
+                out=squares[:], in_=x_sb[v][:, r, :], func=ACT.Square, accum_out=sumsq[:, r, v : v + 1]
             )
+
+        def row_dot(a, b, r, accum):
             products = scratch.tile([P, FEATURES], F32, name="products")
             nc.vector.scalar_tensor_tensor(
-                out=products[:], in0=x_sb[v][:, 1, :], scalar=1.0, in1=x_sb[v][:, 1, :],
-                op0=ALU.mult, op1=ALU.mult, accum_out=sumsq[:, 1, v : v + 1],
+                out=products[:], in0=x_sb[a][:, r, :], scalar=1.0, in1=x_sb[b][:, r, :],
+                op0=ALU.mult, op1=ALU.mult, accum_out=accum,
             )
 
-        x_codes = []
-        x_planes = []
+        grouped_of = {}
+        x_codes = {}
+        x_planes = {}
 
-        def quantise_view(v):
+        def group_view(v):
             grouped = scratch.tile([P, ROWS * P * PACK], BF16, name="grouped", align_bytes=64)
             nc.vector.tensor_copy(
                 out=grouped[:].bitcast(F32).rearrange("p (r b u) -> p r b u", r=ROWS, u=WORD_HALVES),
                 in_=x_t[v][:].rearrange("p r u b -> p r b u"),
             )
+            grouped_of[v] = grouped
+
+        def quantise_view(v):
             codes = keep.tile([P, ROWS * P], U32, name="x_codes%d" % v, align_bytes=64)
             plane = keep.tile([P, ROWS * P], U8, name="x_plane%d" % v, align_bytes=64)
-            nc.vector.quantize_mx(out=codes[:].bitcast(FP8X4), scales=plane[:], in_=grouped[:])
-            x_codes.append(codes)
-            x_planes.append(plane)
+            nc.vector.quantize_mx(out=codes[:].bitcast(FP8X4), scales=plane[:], in_=grouped_of[v][:])
+            x_codes[v] = codes
+            x_planes[v] = plane
 
-        quantise_view(0)
-
-        lengths = keep.tile([P, ROWS, VIEWS], F32, name="lengths")
-        nc.scalar.activation(
-            out=lengths[:], in_=sumsq[:, :, 0:VIEWS], func=ACT.Sqrt, scale=TEMPERATURE
-        )
-        nc.scalar.activation(out=warm[:], in_=one[:], func=ACT.Exp)
         inverse = keep.tile([P, ROWS, VIEWS], F32, name="inverse")
-        nc.vector.reciprocal(out=inverse[:], in_=lengths[:])
-        row_scale = {}
-        for a, b in pair_order:
-            pair_scale = keep.tile([P, ROWS], F32, name="scale%d%d" % (a, b))
-            nc.vector.tensor_tensor(
-                out=pair_scale[:], in0=inverse[:, :, a], in1=inverse[:, :, b], op=ALU.mult
+
+        def inverse_lengths(v0, v1):
+            nc.gpsimd.tensor_tensor(
+                out=inverse[:, :, v0:v1], in0=sumsq[:, :, v0:v1], in1=neg_half[:, :, v0:v1], op=ALU.pow
             )
-            row_scale[(a, b)] = pair_scale
 
-        self_logit = {}
-        for a, b in pair_order:
-            dots = keep.tile([P, ROWS], F32, name="dots%d%d" % (a, b))
+        pair_scale = keep.tile([P, n_pairs, ROWS], F32, name="pair_scale")
+        dots = keep.tile([P, n_pairs, ROWS], F32, name="dots")
+        self_logit = keep.tile([P, n_pairs, ROWS], F32, name="self_logit")
+        self_exp = keep.tile([P, n_pairs, ROWS], F32, name="self_exp")
+
+        def scale_of_pair(k):
+            a, b = pair_order[k]
+            nc.vector.scalar_tensor_tensor(
+                out=pair_scale[:, k, :], in0=inverse[:, :, a], scalar=1.0 / TEMPERATURE,
+                in1=inverse[:, :, b], op0=ALU.mult, op1=ALU.mult,
+            )
+
+        def dots_of_pair(k):
+            a, b = pair_order[k]
             for r in range(ROWS):
-                products = scratch.tile([P, FEATURES], F32, name="products")
-                nc.vector.scalar_tensor_tensor(
-                    out=products[:], in0=x_sb[a][:, r, :], scalar=1.0, in1=x_sb[b][:, r, :],
-                    op0=ALU.mult, op1=ALU.mult, accum_out=dots[:, r : r + 1],
-                )
-            logit = keep.tile([P, ROWS], F32, name="logit%d%d" % (a, b))
-            nc.vector.tensor_tensor(out=logit[:], in0=dots[:], in1=row_scale[(a, b)][:], op=ALU.mult)
-            self_logit[(a, b)] = logit
+                row_dot(a, b, r, dots[:, k, r : r + 1])
 
+        def logits_of_pairs(k0, k1):
+            nc.vector.tensor_tensor(
+                out=self_logit[:, k0:k1, :], in0=dots[:, k0:k1, :], in1=pair_scale[:, k0:k1, :], op=ALU.mult
+            )
+
+        def exp_of_pairs(k0, k1):
+            nc.scalar.activation(out=self_exp[:, k0:k1, :], in_=self_logit[:, k0:k1, :], func=ACT.Exp)
+
+        result_of = []
+        for c in range(len(COMBOS)):
+            result = results.tile([P, ROWS, 1 + BANK_ROWS], F32, name="result")
+            result_of.append(result)
+
+        def pair_index(c):
+            i, j = COMBOS[c]
+            return pair_order.index((min(i, j), max(i, j)))
+
+        def column_zero(k0, k1):
+            for c in range(len(COMBOS)):
+                k = pair_index(c)
+                if k0 <= k < k1:
+                    for r in range(ROWS):
+                        nc.vector.tensor_copy(out=result_of[c][:, r, 0:1], in_=self_exp[:, k, r : r + 1])
+
+        def row_half(c, r):
+            i, j = COMBOS[c]
+            k = pair_index(c)
+            batch_cols = slice(r * P, (r + 1) * P)
+            for n in range(N_TILES):
+                acc = psum_acc.tile([P, N_TILE], F32, name="acc")
+                nc.tensor.matmul_mx(
+                    out=acc[:],
+                    lhsT=x_codes[i][:, batch_cols].bitcast(FP8X4),
+                    lhsT_scale=x_planes[i][:, batch_cols],
+                    rhs=w_sb[(j, n)].bitcast(FP8X4),
+                    rhs_scale=w_planes[j][:, n * N_TILE : (n + 1) * N_TILE],
+                    start=True,
+                    stop=True,
+                )
+                nc.scalar.activation(
+                    out=result_of[c][:, r, 1 + n * N_TILE : 1 + (n + 1) * N_TILE],
+                    in_=acc[:],
+                    func=ACT.Exp,
+                    scale=pair_scale[:, k, r : r + 1],
+                )
+
+        def store_half(c, r):
+            nc.sync.dma_start(
+                out=out[c].rearrange("(p r) q -> p r q", r=ROWS)[:, r, :], in_=result_of[c][:, r, :]
+            )
+
+        transpose_view(0)
+        sumsq_scalar(0, 0)
+        row_dot(0, 0, 1, sumsq[:, 1, 0:1])
+        group_view(0)
+        sumsq_scalar(1, 0)
+        sumsq_scalar(1, 1)
+        quantise_view(0)
+        inverse_lengths(0, 2)
+        scale_of_pair(0)
+        dots_of_pair(0)
+        logits_of_pairs(0, 1)
+
+        row_half(0, 0)
+        exp_of_pairs(0, 1)
+        transpose_view(1)
+
+        for v in (2, 3):
+            for r in range(ROWS):
+                row_dot(v, v, r, sumsq[:, r, v : v + 1])
+            inverse_lengths(v, v + 1)
+        column_zero(0, 1)
+        store_half(0, 0)
+
+        row_half(0, 1)
+        store_half(0, 1)
+        transpose_view(2)
+        transpose_view(3)
+
+        scale_of_pair(1)
+        dots_of_pair(1)
+        for k in range(2, n_pairs):
+            scale_of_pair(k)
+        for k in range(2, n_pairs):
+            dots_of_pair(k)
+        logits_of_pairs(1, n_pairs)
+
+        row_half(1, 0)
+        row_half(1, 1)
+        exp_of_pairs(1, n_pairs)
+        column_zero(1, n_pairs)
+        store_half(1, 0)
+        store_half(1, 1)
+
+        for v in range(1, VIEWS):
+            group_view(v)
         for v in range(1, VIEWS):
             quantise_view(v)
 
-        for c, (i, j) in enumerate(COMBOS):
-            pair = (min(i, j), max(i, j))
-            result = results.tile([P, ROWS, 1 + BANK_ROWS], F32, name="result")
+        for c in range(2, len(COMBOS)):
             for r in range(ROWS):
-                batch_cols = slice(r * P, (r + 1) * P)
-                for n in range(N_TILES):
-                    bank_cols = slice(n * N_TILE, (n + 1) * N_TILE)
-                    acc = psum_acc.tile([P, N_TILE], F32, name="acc")
-                    nc.tensor.matmul_mx(
-                        out=acc[:],
-                        lhsT=x_codes[i][:, batch_cols].bitcast(FP8X4),
-                        lhsT_scale=x_planes[i][:, batch_cols],
-                        rhs=w_sb[j][:, bank_cols].bitcast(FP8X4),
-                        rhs_scale=w_planes[j][:, bank_cols],
-                        start=True,
-                        stop=True,
-                    )
-                    nc.scalar.activation(
-                        out=result[:, r, 1 + n * N_TILE : 1 + (n + 1) * N_TILE],
-                        in_=acc[:],
-                        func=ACT.Exp,
-                        scale=row_scale[pair][:, r : r + 1],
-                    )
-                nc.scalar.activation(
-                    out=result[:, r, 0:1], in_=self_logit[pair][:, r : r + 1], func=ACT.Exp
-                )
-                nc.sync.dma_start(
-                    out=out[c].rearrange("(p r) q -> p r q", r=ROWS)[:, r, :], in_=result[:, r, :]
-                )
+                row_half(c, r)
+                store_half(c, r)

@@ -221,9 +221,15 @@ def tile_memorymoco_pa_kernel(
                 )
 
         def store_half(c, r):
-            nc.sync.dma_start(
-                out=out[c].rearrange("(p r) q -> p r q", r=ROWS)[:, r, :], in_=result_of[c][:, r, :]
-            )
+            if c == len(COMBOS) - 1:
+                nc.sync.dma_start(
+                    out=out[c].rearrange("(p r) q -> p r q", r=ROWS)[:, r, :], in_=result_of[c][:, r, :]
+                )
+            elif r == ROWS - 1:
+                nc.sync.dma_start(
+                    out=out[c].rearrange("(p r) q -> p (r q)", r=ROWS),
+                    in_=result_of[c][:].rearrange("p r q -> p (r q)"),
+                )
 
         transpose_view(0)
         sumsq_scalar(0, 0)

@@ -79,30 +79,31 @@ def tile_memorymoco_pa_kernel(
         w_sb = {}
         w_planes = {}
 
-        def load_bank(j, chunks):
-            plane = keep.tile([P, BANK_ROWS], U8, name="w_plane%d" % j, align_bytes=64)
-            plane_i32 = plane[:].bitcast(I32)
-            nc.vector.memset(plane_i32, 0)
-            rows_by_s = bank_scales[j][0].rearrange("(q s) n -> s q n", s=SCALE_ROWS)
-            for s in range(SCALE_ROWS):
-                nc.sync.dma_start(out=plane_i32[s : P : QUADRANT, :], in_=rows_by_s[s].bitcast(I32))
-            w_planes[j] = plane
-            words = bank_words[j][0].rearrange("p n t -> p (n t)").bitcast(I32)
-            first = 0
-            for tiles in chunks:
-                w_tile = keep.tile([P, tiles * N_TILE], I32, name="w%d_%d" % (j, first), align_bytes=64)
-                nc.sync.dma_start(out=w_tile[:], in_=words[:, first * N_TILE : (first + tiles) * N_TILE])
-                for n in range(tiles):
-                    w_sb[(j, first + n)] = w_tile[:, n * N_TILE : (n + 1) * N_TILE]
-                first += tiles
+        def load_bank(j):
+            planes = keep.tile([P, N_TILE], U8, name="w_planes%d" % j, align_bytes=64)
+            planes_i32 = planes[:].bitcast(I32)
+            nc.vector.memset(planes_i32, 0)
+            rows = bank_scales[j][0].bitcast(I32).rearrange(
+                "(q s) (n w) -> q n s w", s=SCALE_ROWS, n=N_TILES
+            )
+            for q in range(P // QUADRANT):
+                nc.sync.dma_start(
+                    out=planes_i32[q * QUADRANT : q * QUADRANT + N_TILES * SCALE_ROWS, :], in_=rows[q]
+                )
+            w_planes[j] = planes
+            w_tile = keep.tile([P, BANK_ROWS], I32, name="w%d" % j, align_bytes=64)
+            nc.sync.dma_start(
+                out=w_tile[:], in_=bank_words[j][0].rearrange("p n t -> p (n t)").bitcast(I32)
+            )
+            w_sb[j] = w_tile
 
         load_view(0)
         load_view(1)
-        load_bank(bank_order[0], (1, 1, 2))
+        load_bank(bank_order[0])
         load_view(2)
         load_view(3)
         for j in bank_order[1:]:
-            load_bank(j, (N_TILES,))
+            load_bank(j)
 
         x_t = {}
 
@@ -208,8 +209,8 @@ def tile_memorymoco_pa_kernel(
                     out=acc[:],
                     lhsT=x_codes[i][:, batch_cols].bitcast(FP8X4),
                     lhsT_scale=x_planes[i][:, batch_cols],
-                    rhs=w_sb[(j, n)].bitcast(FP8X4),
-                    rhs_scale=w_planes[j][:, n * N_TILE : (n + 1) * N_TILE],
+                    rhs=w_sb[j][:, n * N_TILE : (n + 1) * N_TILE].bitcast(FP8X4),
+                    rhs_scale=w_planes[j][n * SCALE_ROWS : P, :],
                     start=True,
                     stop=True,
                 )

@@ -222,12 +222,9 @@ def tile_memorymoco_pa_kernel(
                 )
 
         def store_half(c, r):
-            if c == len(COMBOS) - 1:
-                nc.sync.dma_start(
-                    out=out[c].rearrange("(p r) q -> p r q", r=ROWS)[:, r, :], in_=result_of[c][:, r, :]
-                )
-            elif r == ROWS - 1:
-                nc.sync.dma_start(
+            if r == ROWS - 1:
+                queue = nc.scalar if c % 2 == 0 else nc.sync
+                queue.dma_start(
                     out=out[c].rearrange("(p r) q -> p (r q)", r=ROWS),
                     in_=result_of[c][:].rearrange("p r q -> p (r q)"),
                 )

from contextlib import ExitStack

import concourse.mybir as mybir
from concourse.masks import make_identity

F32 = mybir.dt.float32
BF16 = mybir.dt.bfloat16
I32 = mybir.dt.int32
U32 = mybir.dt.uint32
U8 = mybir.dt.uint8
FP8X4 = mybir.dt.float8_e4m3fn_x4
ACT = mybir.ActivationFunctionType
ALU = mybir.AluOpType

P = 128
BATCH, BANK_ROWS, FEATURES = 256, 2048, 512
VIEWS = 4
COMBOS = ((0, 1), (0, 2), (0, 3), (1, 0), (1, 2), (2, 0), (2, 1), (3, 0))
TEMPERATURE = 0.07

ROWS = BATCH // P
PACK = 4
WORD_HALVES = 2
N_TILE = 512
N_TILES = BANK_ROWS // N_TILE
QUADRANT = 32
SCALE_ROWS = 4
BLOCK_F32 = 8

FLOPS = 2 * len(COMBOS) * BATCH * BANK_ROWS * FEATURES


def tile_memorymoco_pa_kernel(
    tc,
    x0, x1, x2, x3,
    mem0_words, mem0_scales, mem1_words, mem1_scales,
    mem2_words, mem2_scales, mem3_words, mem3_scales,
    out,
):
    nc = tc.nc
    views = (x0, x1, x2, x3)
    bank_words = (mem0_words, mem1_words, mem2_words, mem3_words)
    bank_scales = (mem0_scales, mem1_scales, mem2_scales, mem3_scales)

    bank_order = []
    pair_order = []
    for i, j in COMBOS:
        if j not in bank_order:
            bank_order.append(j)
        if (min(i, j), max(i, j)) not in pair_order:
            pair_order.append((min(i, j), max(i, j)))
    n_pairs = len(pair_order)

    with ExitStack() as ctx:
        keep = ctx.enter_context(tc.tile_pool(name="keep", bufs=1))
        scratch = ctx.enter_context(tc.tile_pool(name="scratch", bufs=4))
        results = ctx.enter_context(tc.tile_pool(name="results", bufs=len(COMBOS)))
        psum_x = ctx.enter_context(tc.psum_pool(name="psum_x", bufs=VIEWS))
        psum_acc = ctx.enter_context(tc.psum_pool(name="psum_acc", bufs=4))
        ctx.enter_context(tc.manual_schedule())

        one = keep.tile([P, 1], F32, name="one")
        nc.vector.memset(one[:], 1.0)
        warm = keep.tile([P, 1], F32, name="warm")
        nc.scalar.activation(out=warm[:], in_=one[:], func=ACT.Exp)
        neg_half = keep.tile([P, ROWS, VIEWS], F32, name="neg_half")
        nc.vector.memset(neg_half[:], -0.5)

        ident = keep.tile([P, P], F32, name="ident")
        make_identity(nc, ident[:])

        x_sb = {}

        def load_view(v):
            x_tile = keep.tile([P, ROWS, FEATURES], BF16, name="x%d" % v)
            nc.sync.dma_start(out=x_tile[:], in_=views[v].rearrange("(p r) d -> p r d", r=ROWS))
            x_sb[v] = x_tile

        w_sb = {}
        w_planes = {}

        def load_bank(j):
            planes = keep.tile([P, N_TILE], U8, name="w_planes%d" % j, align_bytes=64)
            planes_i32 = planes[:].bitcast(I32)
            nc.vector.memset(planes_i32, 0)
            rows = bank_scales[j][0].bitcast(I32).rearrange(
                "(q s) (n w) -> q n s w", s=SCALE_ROWS, n=N_TILES
            )
            for q in range(P // QUADRANT):
                nc.sync.dma_start(
                    out=planes_i32[q * QUADRANT : q * QUADRANT + N_TILES * SCALE_ROWS, :], in_=rows[q]
                )
            w_planes[j] = planes
            w_tile = keep.tile([P, BANK_ROWS], I32, name="w%d" % j, align_bytes=64)
            nc.sync.dma_start(
                out=w_tile[:], in_=bank_words[j][0].rearrange("p n t -> p (n t)").bitcast(I32)
            )
            w_sb[j] = w_tile

        load_view(0)
        load_view(1)
        load_bank(bank_order[0])
        load_view(2)
        load_view(3)
        for j in bank_order[1:]:
            load_bank(j)

        x_t = {}

        def transpose_view(v):
            xt = psum_x.tile([P, ROWS, WORD_HALVES, P], F32, name="xt")
            x_words = x_sb[v][:].bitcast(F32)
            for r in range(ROWS):
                for u in range(WORD_HALVES):
                    nc.tensor.transpose(
                        xt[:, r, u, :], x_words[:, r, u : FEATURES // 2 : WORD_HALVES], ident[:]
                    )
            x_t[v] = xt

        sumsq = keep.tile([P, ROWS, BLOCK_F32], F32, name="sumsq")

        def sumsq_scalar(v, r):
            squares = scratch.tile([P, FEATURES], F32, name="squares")
            nc.scalar.activation(
                out=squares[:], in_=x_sb[v][:, r, :], func=ACT.Square, accum_out=sumsq[:, r, v : v + 1]
            )

        def row_dot(a, b, r, accum):
            products = scratch.tile([P, FEATURES], F32, name="products")
            nc.vector.scalar_tensor_tensor(
                out=products[:], in0=x_sb[a][:, r, :], scalar=1.0, in1=x_sb[b][:, r, :],
                op0=ALU.mult, op1=ALU.mult, accum_out=accum,
            )

        grouped_of = {}
        x_codes = {}
        x_planes = {}

        def group_view(v):
            grouped = scratch.tile([P, ROWS * P * PACK], BF16, name="grouped", align_bytes=64)
            nc.vector.tensor_copy(
                out=grouped[:].bitcast(F32).rearrange("p (r b u) -> p r b u", r=ROWS, u=WORD_HALVES),
                in_=x_t[v][:].rearrange("p r u b -> p r b u"),
            )
            grouped_of[v] = grouped

        def quantise_view(v):
            codes = keep.tile([P, ROWS * P], U32, name="x_codes%d" % v, align_bytes=64)
            plane = keep.tile([P, ROWS * P], U8, name="x_plane%d" % v, align_bytes=64)
            nc.vector.quantize_mx(out=codes[:].bitcast(FP8X4), scales=plane[:], in_=grouped_of[v][:])
            x_codes[v] = codes
            x_planes[v] = plane

        inverse = keep.tile([P, ROWS, VIEWS], F32, name="inverse")

        def inverse_lengths(v0, v1):
            nc.gpsimd.tensor_tensor(
                out=inverse[:, :, v0:v1], in0=sumsq[:, :, v0:v1], in1=neg_half[:, :, v0:v1], op=ALU.pow
            )

        pair_scale = keep.tile([P, n_pairs, ROWS], F32, name="pair_scale")
        dots = keep.tile([P, n_pairs, ROWS], F32, name="dots")
        self_logit = keep.tile([P, n_pairs, ROWS], F32, name="self_logit")
        self_exp = keep.tile([P, n_pairs, ROWS], F32, name="self_exp")

        def scale_of_pair(k):
            a, b = pair_order[k]
            nc.vector.scalar_tensor_tensor(
                out=pair_scale[:, k, :], in0=inverse[:, :, a], scalar=1.0 / TEMPERATURE,
                in1=inverse[:, :, b], op0=ALU.mult, op1=ALU.mult,
            )

        def dots_of_pair(k):
            a, b = pair_order[k]
            for r in range(ROWS):
                row_dot(a, b, r, dots[:, k, r : r + 1])

        def logits_of_pairs(k0, k1):
            nc.vector.tensor_tensor(
                out=self_logit[:, k0:k1, :], in0=dots[:, k0:k1, :], in1=pair_scale[:, k0:k1, :], op=ALU.mult
            )

        def exp_of_pairs(k0, k1):
            nc.scalar.activation(out=self_exp[:, k0:k1, :], in_=self_logit[:, k0:k1, :], func=ACT.Exp)

        result_of = []
        for c in range(len(COMBOS)):
            result = results.tile([P, ROWS, 1 + BANK_ROWS], F32, name="result")
            result_of.append(result)

        def pair_index(c):
            i, j = COMBOS[c]
            return pair_order.index((min(i, j), max(i, j)))

        def column_zero(k0, k1):
            for c in range(len(COMBOS)):
                k = pair_index(c)
                if k0 <= k < k1:
                    for r in range(ROWS):
                        nc.vector.tensor_copy(out=result_of[c][:, r, 0:1], in_=self_exp[:, k, r : r + 1])

        def row_half(c, r):
            i, j = COMBOS[c]
            k = pair_index(c)
            batch_cols = slice(r * P, (r + 1) * P)
            for n in range(N_TILES):
                acc = psum_acc.tile([P, N_TILE], F32, name="acc")
                nc.tensor.matmul_mx(
                    out=acc[:],
                    lhsT=x_codes[i][:, batch_cols].bitcast(FP8X4),
                    lhsT_scale=x_planes[i][:, batch_cols],
                    rhs=w_sb[j][:, n * N_TILE : (n + 1) * N_TILE].bitcast(FP8X4),
                    rhs_scale=w_planes[j][n * SCALE_ROWS : P, :],
                    start=True,
                    stop=True,
                )
                nc.scalar.activation(
                    out=result_of[c][:, r, 1 + n * N_TILE : 1 + (n + 1) * N_TILE],
                    in_=acc[:],
                    func=ACT.Exp,
                    scale=pair_scale[:, k, r : r + 1],
                )

        def store_half(c, r):
            if r == ROWS - 1:
                queue = nc.scalar if c % 2 == 0 else nc.sync
                queue.dma_start(
                    out=out[c].rearrange("(p r) q -> p (r q)", r=ROWS),
                    in_=result_of[c][:].rearrange("p r q -> p (r q)"),
                )

        transpose_view(0)
        sumsq_scalar(0, 0)
        row_dot(0, 0, 1, sumsq[:, 1, 0:1])
        group_view(0)
        sumsq_scalar(1, 0)
        sumsq_scalar(1, 1)
        quantise_view(0)
        inverse_lengths(0, 2)
        scale_of_pair(0)
        dots_of_pair(0)
        logits_of_pairs(0, 1)

        row_half(0, 0)
        exp_of_pairs(0, 1)
        transpose_view(1)

        for v in (2, 3):
            for r in range(ROWS):
                row_dot(v, v, r, sumsq[:, r, v : v + 1])
            inverse_lengths(v, v + 1)
        column_zero(0, 1)
        store_half(0, 0)

        row_half(0, 1)
        store_half(0, 1)
        transpose_view(2)
        transpose_view(3)

        scale_of_pair(1)
        dots_of_pair(1)
        for k in range(2, n_pairs):
            scale_of_pair(k)
        for k in range(2, n_pairs):
            dots_of_pair(k)
        logits_of_pairs(1, n_pairs)

        row_half(1, 0)
        row_half(1, 1)
        exp_of_pairs(1, n_pairs)
        column_zero(1, n_pairs)
        store_half(1, 0)
        store_half(1, 1)

        for v in range(1, VIEWS):
            group_view(v)
        for v in range(1, VIEWS):
            quantise_view(v)

        for c in range(2, len(COMBOS)):
            for r in range(ROWS):
                row_half(c, r)
                store_half(c, r)
